import numpy as np
import ml_dtypes

BF16 = ml_dtypes.bfloat16


def bf(x):
    return np.asarray(x, np.float32).astype(BF16)


def f32(x):
    return np.asarray(x, np.float32)


def f64(x):
    return np.asarray(x).astype(np.float64)


def striped(idx):
    return np.tile(idx.reshape(-1, 16).T, (8, 1))


C, V, B, T, N = 256, 2048, 4, 256, 1024


def setup_inputs():
    return {'tok': f32(np.random.standard_normal((C, V))), 'pos': f32(np.random.standard_normal((C, T))), 'typ': f32(0.5 * np.random.standard_normal((C, 1))), 'offs': striped(np.random.permutation(np.tile(np.arange(V), 2))[:N])}


def reference(tok, pos, typ, offs):
    idx = offs[:16].T.reshape(-1)
    return f64(tok)[:, idx] + np.tile(f64(pos), (1, B)) + f64(typ)

@@ -1,0 +1,47 @@
+import concourse.mybir as mybir
+
+F32 = mybir.dt.float32
+U16 = mybir.dt.uint16
+ADD = mybir.AluOpType.add
+
+P = 128
+CHANNELS = 256
+VOCAB = 2048
+SEQ_LEN = 256
+SEQUENCES = 4
+TOKENS = SEQUENCES * SEQ_LEN
+OFFS_PER_COL = 16
+SEQ_COLS = SEQ_LEN // OFFS_PER_COL
+
+
+def tile_enhancedtransformertextclassifier_kernel(tc, tok, pos, typ, offs, out):
+    nc = tc.nc
+    with (
+        tc.tile_pool(name="held", bufs=1) as held,
+        tc.tile_pool(name="results", bufs=4) as results,
+    ):
+        offsets = held.tile([P, TOKENS // OFFS_PER_COL], U16, name="offsets")
+        nc.sync.dma_start(offsets[:], offs)
+
+        for block in range(CHANNELS // P):
+            channels = slice(block * P, (block + 1) * P)
+
+            table = held.tile([P, VOCAB], F32, name=f"table{block}")
+            nc.sync.dma_start(table[:], tok[channels, :])
+
+            position = held.tile([P, SEQ_LEN], F32, name=f"position{block}")
+            nc.scalar.dma_start(position[:], pos[channels, :])
+            token_type = held.tile([P, 1], F32, name=f"token_type{block}")
+            nc.scalar.dma_start(token_type[:], typ[channels, :])
+            positional = held.tile([P, SEQ_LEN], F32, name=f"positional{block}")
+            nc.vector.tensor_scalar_add(positional[:], position[:], token_type[:, 0:1])
+
+            for seq in range(SEQUENCES):
+                embedded = results.tile([P, SEQ_LEN], F32, name="embedded")
+                nc.vector.tensor_tensor(
+                    embedded[:],
+                    table[:].indirect(offsets[:, seq * SEQ_COLS : (seq + 1) * SEQ_COLS]),
+                    positional[:],
+                    ADD,
+                )
+                nc.scalar.dma_start(out[channels, seq * SEQ_LEN : (seq + 1) * SEQ_LEN], embedded[:])

@@ -44,4 +44,4 @@ def tile_enhancedtransformertextclassifier_kernel(tc, tok, pos, typ, offs, out):
                     positional[:],
                     ADD,
                 )
-                nc.scalar.dma_start(out[channels, seq * SEQ_LEN : (seq + 1) * SEQ_LEN], embedded[:])
+                nc.sync.dma_start(out[channels, seq * SEQ_LEN : (seq + 1) * SEQ_LEN], embedded[:])

@@ -27,7 +27,11 @@ def tile_enhancedtransformertextclassifier_kernel(tc, tok, pos, typ, offs, out):
             channels = slice(block * P, (block + 1) * P)
 
             table = held.tile([P, VOCAB], F32, name=f"table{block}")
-            nc.sync.dma_start(table[:], tok[channels, :])
+            pieces = 4 if block == 0 else 1
+            width = VOCAB // pieces
+            for piece in range(pieces):
+                words = slice(piece * width, (piece + 1) * width)
+                nc.sync.dma_start(table[:, words], tok[channels, words])
 
             position = held.tile([P, SEQ_LEN], F32, name=f"position{block}")
             nc.scalar.dma_start(position[:], pos[channels, :])
@@ -44,4 +48,4 @@ def tile_enhancedtransformertextclassifier_kernel(tc, tok, pos, typ, offs, out):
                     positional[:],
                     ADD,
                 )
-                nc.sync.dma_start(out[channels, seq * SEQ_LEN : (seq + 1) * SEQ_LEN], embedded[:])
+                nc.scalar.dma_start(out[channels, seq * SEQ_LEN : (seq + 1) * SEQ_LEN], embedded[:])

@@ -37,15 +37,21 @@ def tile_enhancedtransformertextclassifier_kernel(tc, tok, pos, typ, offs, out):
             nc.scalar.dma_start(position[:], pos[channels, :])
             token_type = held.tile([P, 1], F32, name=f"token_type{block}")
             nc.scalar.dma_start(token_type[:], typ[channels, :])
-            positional = held.tile([P, SEQ_LEN], F32, name=f"positional{block}")
-            nc.vector.tensor_scalar_add(positional[:], position[:], token_type[:, 0:1])
 
-            for seq in range(SEQUENCES):
-                embedded = results.tile([P, SEQ_LEN], F32, name="embedded")
+            group = SEQUENCES if block == 0 else 1
+
+            positional = held.tile([P, group * SEQ_LEN], F32, name=f"positional{block}")
+            for seq in range(group):
+                nc.vector.tensor_scalar_add(
+                    positional[:, seq * SEQ_LEN : (seq + 1) * SEQ_LEN], position[:], token_type[:, 0:1]
+                )
+
+            for first in range(0, SEQUENCES, group):
+                embedded = results.tile([P, group * SEQ_LEN], F32, name=f"embedded{group}")
                 nc.vector.tensor_tensor(
                     embedded[:],
-                    table[:].indirect(offsets[:, seq * SEQ_COLS : (seq + 1) * SEQ_COLS]),
+                    table[:].indirect(offsets[:, first * SEQ_COLS : (first + group) * SEQ_COLS]),
                     positional[:],
                     ADD,
                 )
-                nc.scalar.dma_start(out[channels, seq * SEQ_LEN : (seq + 1) * SEQ_LEN], embedded[:])
+                nc.scalar.dma_start(out[channels, first * SEQ_LEN : (first + group) * SEQ_LEN], embedded[:])

@@ -3,9 +3,11 @@ import concourse.mybir as mybir
 F32 = mybir.dt.float32
 U16 = mybir.dt.uint16
 ADD = mybir.AluOpType.add
+IDENTITY = mybir.ActivationFunctionType.Identity
 
 P = 128
 CHANNELS = 256
+BLOCKS = CHANNELS // P
 VOCAB = 2048
 SEQ_LEN = 256
 SEQUENCES = 4
@@ -16,15 +18,13 @@ SEQ_COLS = SEQ_LEN // OFFS_PER_COL
 
 def tile_enhancedtransformertextclassifier_kernel(tc, tok, pos, typ, offs, out):
     nc = tc.nc
-    with (
-        tc.tile_pool(name="held", bufs=1) as held,
-        tc.tile_pool(name="results", bufs=4) as results,
-    ):
+    with tc.tile_pool(name="held", bufs=1) as held:
         offsets = held.tile([P, TOKENS // OFFS_PER_COL], U16, name="offsets")
         nc.sync.dma_start(offsets[:], offs)
 
-        for block in range(CHANNELS // P):
+        for block in range(BLOCKS):
             channels = slice(block * P, (block + 1) * P)
+            last_block = block == BLOCKS - 1
 
             table = held.tile([P, VOCAB], F32, name=f"table{block}")
             pieces = 4 if block == 0 else 1
@@ -38,20 +38,25 @@ def tile_enhancedtransformertextclassifier_kernel(tc, tok, pos, typ, offs, out):
             token_type = held.tile([P, 1], F32, name=f"token_type{block}")
             nc.scalar.dma_start(token_type[:], typ[channels, :])
 
-            group = SEQUENCES if block == 0 else 1
+            groups = [SEQUENCES - 1, 1] if last_block else [SEQUENCES]
 
-            positional = held.tile([P, group * SEQ_LEN], F32, name=f"positional{block}")
-            for seq in range(group):
-                nc.vector.tensor_scalar_add(
-                    positional[:, seq * SEQ_LEN : (seq + 1) * SEQ_LEN], position[:], token_type[:, 0:1]
-                )
+            positional = held.tile([P, max(groups) * SEQ_LEN], F32, name=f"positional{block}")
+            for seq in range(max(groups)):
+                copy_of_term = positional[:, seq * SEQ_LEN : (seq + 1) * SEQ_LEN]
+                if block == 0:
+                    nc.vector.tensor_scalar_add(copy_of_term, position[:], token_type[:, 0:1])
+                else:
+                    nc.scalar.activation(copy_of_term, position[:], IDENTITY, bias=token_type[:, 0:1])
 
-            for first in range(0, SEQUENCES, group):
-                embedded = results.tile([P, group * SEQ_LEN], F32, name=f"embedded{group}")
+            embedded = held.tile([P, TOKENS], F32, name=f"embedded{block}")
+            first = 0
+            for group in groups:
+                tokens = slice(first * SEQ_LEN, (first + group) * SEQ_LEN)
                 nc.vector.tensor_tensor(
-                    embedded[:],
+                    embedded[:, tokens],
                     table[:].indirect(offsets[:, first * SEQ_COLS : (first + group) * SEQ_COLS]),
-                    positional[:],
+                    positional[:, 0 : group * SEQ_LEN],
                     ADD,
                 )
-                nc.scalar.dma_start(out[channels, first * SEQ_LEN : (first + group) * SEQ_LEN], embedded[:])
+                nc.scalar.dma_start(out[channels, tokens], embedded[:, tokens])
+                first += group

@@ -3,11 +3,9 @@ import concourse.mybir as mybir
 F32 = mybir.dt.float32
 U16 = mybir.dt.uint16
 ADD = mybir.AluOpType.add
-IDENTITY = mybir.ActivationFunctionType.Identity
 
 P = 128
 CHANNELS = 256
-BLOCKS = CHANNELS // P
 VOCAB = 2048
 SEQ_LEN = 256
 SEQUENCES = 4
@@ -18,16 +16,18 @@ SEQ_COLS = SEQ_LEN // OFFS_PER_COL
 
 def tile_enhancedtransformertextclassifier_kernel(tc, tok, pos, typ, offs, out):
     nc = tc.nc
-    with tc.tile_pool(name="held", bufs=1) as held:
+    with (
+        tc.tile_pool(name="held", bufs=1) as held,
+        tc.tile_pool(name="results", bufs=4) as results,
+    ):
         offsets = held.tile([P, TOKENS // OFFS_PER_COL], U16, name="offsets")
         nc.sync.dma_start(offsets[:], offs)
 
-        for block in range(BLOCKS):
+        for block in range(CHANNELS // P):
             channels = slice(block * P, (block + 1) * P)
-            last_block = block == BLOCKS - 1
 
             table = held.tile([P, VOCAB], F32, name=f"table{block}")
-            pieces = 4 if block == 0 else 1
+            pieces = 4
             width = VOCAB // pieces
             for piece in range(pieces):
                 words = slice(piece * width, (piece + 1) * width)
@@ -38,25 +38,20 @@ def tile_enhancedtransformertextclassifier_kernel(tc, tok, pos, typ, offs, out):
             token_type = held.tile([P, 1], F32, name=f"token_type{block}")
             nc.scalar.dma_start(token_type[:], typ[channels, :])
 
-            groups = [SEQUENCES - 1, 1] if last_block else [SEQUENCES]
+            group = SEQUENCES if block == 0 else 1
 
-            positional = held.tile([P, max(groups) * SEQ_LEN], F32, name=f"positional{block}")
-            for seq in range(max(groups)):
-                copy_of_term = positional[:, seq * SEQ_LEN : (seq + 1) * SEQ_LEN]
-                if block == 0:
-                    nc.vector.tensor_scalar_add(copy_of_term, position[:], token_type[:, 0:1])
-                else:
-                    nc.scalar.activation(copy_of_term, position[:], IDENTITY, bias=token_type[:, 0:1])
+            positional = held.tile([P, group * SEQ_LEN], F32, name=f"positional{block}")
+            for seq in range(group):
+                nc.vector.tensor_scalar_add(
+                    positional[:, seq * SEQ_LEN : (seq + 1) * SEQ_LEN], position[:], token_type[:, 0:1]
+                )
 
-            embedded = held.tile([P, TOKENS], F32, name=f"embedded{block}")
-            first = 0
-            for group in groups:
-                tokens = slice(first * SEQ_LEN, (first + group) * SEQ_LEN)
+            for first in range(0, SEQUENCES, group):
+                embedded = results.tile([P, group * SEQ_LEN], F32, name=f"embedded{group}")
                 nc.vector.tensor_tensor(
-                    embedded[:, tokens],
+                    embedded[:],
                     table[:].indirect(offsets[:, first * SEQ_COLS : (first + group) * SEQ_COLS]),
-                    positional[:, 0 : group * SEQ_LEN],
+                    positional[:],
                     ADD,
                 )
-                nc.scalar.dma_start(out[channels, tokens], embedded[:, tokens])
-                first += group
+                nc.scalar.dma_start(out[channels, first * SEQ_LEN : (first + group) * SEQ_LEN], embedded[:])

@@ -6,6 +6,7 @@ ADD = mybir.AluOpType.add
 
 P = 128
 CHANNELS = 256
+BLOCKS = CHANNELS // P
 VOCAB = 2048
 SEQ_LEN = 256
 SEQUENCES = 4
@@ -16,18 +17,16 @@ SEQ_COLS = SEQ_LEN // OFFS_PER_COL
 
 def tile_enhancedtransformertextclassifier_kernel(tc, tok, pos, typ, offs, out):
     nc = tc.nc
-    with (
-        tc.tile_pool(name="held", bufs=1) as held,
-        tc.tile_pool(name="results", bufs=4) as results,
-    ):
+    with tc.tile_pool(name="held", bufs=1) as held:
         offsets = held.tile([P, TOKENS // OFFS_PER_COL], U16, name="offsets")
         nc.sync.dma_start(offsets[:], offs)
 
-        for block in range(CHANNELS // P):
+        for block in range(BLOCKS):
             channels = slice(block * P, (block + 1) * P)
+            last_block = block == BLOCKS - 1
 
             table = held.tile([P, VOCAB], F32, name=f"table{block}")
-            pieces = 4
+            pieces = 4 if block == 0 else 1
             width = VOCAB // pieces
             for piece in range(pieces):
                 words = slice(piece * width, (piece + 1) * width)
@@ -38,20 +37,25 @@ def tile_enhancedtransformertextclassifier_kernel(tc, tok, pos, typ, offs, out):
             token_type = held.tile([P, 1], F32, name=f"token_type{block}")
             nc.scalar.dma_start(token_type[:], typ[channels, :])
 
-            group = SEQUENCES if block == 0 else 1
+            groups = [SEQUENCES - 1, 1] if last_block else [SEQUENCES]
 
-            positional = held.tile([P, group * SEQ_LEN], F32, name=f"positional{block}")
-            for seq in range(group):
-                nc.vector.tensor_scalar_add(
-                    positional[:, seq * SEQ_LEN : (seq + 1) * SEQ_LEN], position[:], token_type[:, 0:1]
-                )
+            copies = max(groups)
+            positional = held.tile([P, copies, SEQ_LEN], F32, name=f"positional{block}")
+            nc.vector.tensor_scalar_add(
+                positional[:],
+                position[:].unsqueeze(1).to_broadcast([P, copies, SEQ_LEN]),
+                token_type[:, 0:1],
+            )
 
-            for first in range(0, SEQUENCES, group):
-                embedded = results.tile([P, group * SEQ_LEN], F32, name=f"embedded{group}")
+            embedded = held.tile([P, TOKENS], F32, name=f"embedded{block}")
+            first = 0
+            for group in groups:
+                tokens = slice(first * SEQ_LEN, (first + group) * SEQ_LEN)
                 nc.vector.tensor_tensor(
-                    embedded[:],
+                    embedded[:, tokens],
                     table[:].indirect(offsets[:, first * SEQ_COLS : (first + group) * SEQ_COLS]),
-                    positional[:],
+                    positional[:, 0:group, :].rearrange("p s t -> p (s t)"),
                     ADD,
                 )
-                nc.scalar.dma_start(out[channels, first * SEQ_LEN : (first + group) * SEQ_LEN], embedded[:])
+                nc.scalar.dma_start(out[channels, tokens], embedded[:, tokens])
+                first += group

@@ -6,7 +6,6 @@ ADD = mybir.AluOpType.add
 
 P = 128
 CHANNELS = 256
-BLOCKS = CHANNELS // P
 VOCAB = 2048
 SEQ_LEN = 256
 SEQUENCES = 4
@@ -14,16 +13,26 @@ TOKENS = SEQUENCES * SEQ_LEN
 OFFS_PER_COL = 16
 SEQ_COLS = SEQ_LEN // OFFS_PER_COL
 
+FLOPS = 2 * CHANNELS * TOKENS
+
 
 def tile_enhancedtransformertextclassifier_kernel(tc, tok, pos, typ, offs, out):
     nc = tc.nc
-    with tc.tile_pool(name="held", bufs=1) as held:
+    with (
+        tc.tile_pool(name="held", bufs=1) as held,
+        tc.tile_pool(name="results", bufs=4) as results,
+        tc.psum_pool(name="psum", bufs=1) as psum,
+    ):
         offsets = held.tile([P, TOKENS // OFFS_PER_COL], U16, name="offsets")
         nc.sync.dma_start(offsets[:], offs)
 
-        for block in range(BLOCKS):
+        type_row = held.tile([1, CHANNELS], F32, name="type_row")
+        nc.scalar.dma_start(type_row[:], typ.rearrange("c o -> o c"))
+        one = held.tile([1, 1], F32, name="one")
+        nc.vector.memset(one[:], 1.0)
+
+        for block in range(CHANNELS // P):
             channels = slice(block * P, (block + 1) * P)
-            last_block = block == BLOCKS - 1
 
             table = held.tile([P, VOCAB], F32, name=f"table{block}")
             pieces = 4 if block == 0 else 1
@@ -34,28 +43,23 @@ def tile_enhancedtransformertextclassifier_kernel(tc, tok, pos, typ, offs, out):
 
             position = held.tile([P, SEQ_LEN], F32, name=f"position{block}")
             nc.scalar.dma_start(position[:], pos[channels, :])
-            token_type = held.tile([P, 1], F32, name=f"token_type{block}")
-            nc.scalar.dma_start(token_type[:], typ[channels, :])
+            token_type = psum.tile([P, 1], F32, name=f"token_type{block}")
+            nc.tensor.matmul(token_type[:], type_row[:, channels], one[:], start=True, stop=True)
 
-            groups = [SEQUENCES - 1, 1] if last_block else [SEQUENCES]
+            group = SEQUENCES if block == 0 else 1
 
-            copies = max(groups)
-            positional = held.tile([P, copies, SEQ_LEN], F32, name=f"positional{block}")
-            nc.vector.tensor_scalar_add(
-                positional[:],
-                position[:].unsqueeze(1).to_broadcast([P, copies, SEQ_LEN]),
-                token_type[:, 0:1],
-            )
+            positional = held.tile([P, group * SEQ_LEN], F32, name=f"positional{block}")
+            for seq in range(group):
+                nc.vector.tensor_scalar_add(
+                    positional[:, seq * SEQ_LEN : (seq + 1) * SEQ_LEN], position[:], token_type[:, 0:1]
+                )
 
-            embedded = held.tile([P, TOKENS], F32, name=f"embedded{block}")
-            first = 0
-            for group in groups:
-                tokens = slice(first * SEQ_LEN, (first + group) * SEQ_LEN)
+            for first in range(0, SEQUENCES, group):
+                embedded = results.tile([P, group * SEQ_LEN], F32, name=f"embedded{group}")
                 nc.vector.tensor_tensor(
-                    embedded[:, tokens],
+                    embedded[:],
                     table[:].indirect(offsets[:, first * SEQ_COLS : (first + group) * SEQ_COLS]),
-                    positional[:, 0:group, :].rearrange("p s t -> p (s t)"),
+                    positional[:],
                     ADD,
                 )
-                nc.scalar.dma_start(out[channels, tokens], embedded[:, tokens])
-                first += group
+                nc.scalar.dma_start(out[channels, first * SEQ_LEN : (first + group) * SEQ_LEN], embedded[:])

@@ -6,6 +6,7 @@ ADD = mybir.AluOpType.add
 
 P = 128
 CHANNELS = 256
+BLOCKS = CHANNELS // P
 VOCAB = 2048
 SEQ_LEN = 256
 SEQUENCES = 4
@@ -15,12 +16,15 @@ SEQ_COLS = SEQ_LEN // OFFS_PER_COL
 
 FLOPS = 2 * CHANNELS * TOKENS
 
+PIECES = [[TOKENS], [TOKENS // 2, TOKENS // 4, TOKENS // 8, TOKENS // 16, TOKENS // 16]]
+TABLE_LOADS = [4, 1]
+
 
 def tile_enhancedtransformertextclassifier_kernel(tc, tok, pos, typ, offs, out):
     nc = tc.nc
     with (
         tc.tile_pool(name="held", bufs=1) as held,
-        tc.tile_pool(name="results", bufs=4) as results,
+        tc.tile_pool(name="results", bufs=1) as results,
         tc.psum_pool(name="psum", bufs=1) as psum,
     ):
         offsets = held.tile([P, TOKENS // OFFS_PER_COL], U16, name="offsets")
@@ -31,35 +35,38 @@ def tile_enhancedtransformertextclassifier_kernel(tc, tok, pos, typ, offs, out):
         one = held.tile([1, 1], F32, name="one")
         nc.vector.memset(one[:], 1.0)
 
-        for block in range(CHANNELS // P):
+        for block in range(BLOCKS):
             channels = slice(block * P, (block + 1) * P)
 
             table = held.tile([P, VOCAB], F32, name=f"table{block}")
-            pieces = 4 if block == 0 else 1
-            width = VOCAB // pieces
-            for piece in range(pieces):
-                words = slice(piece * width, (piece + 1) * width)
+            width = VOCAB // TABLE_LOADS[block]
+            for load in range(TABLE_LOADS[block]):
+                words = slice(load * width, (load + 1) * width)
                 nc.sync.dma_start(table[:, words], tok[channels, words])
 
-            position = held.tile([P, SEQ_LEN], F32, name=f"position{block}")
-            nc.scalar.dma_start(position[:], pos[channels, :])
-            token_type = psum.tile([P, 1], F32, name=f"token_type{block}")
-            nc.tensor.matmul(token_type[:], type_row[:, channels], one[:], start=True, stop=True)
+            position_tile = held.tile([P, SEQ_LEN], F32, name=f"position{block}")
+            nc.scalar.dma_start(position_tile[:], pos[channels, :])
+            position = position_tile[:]
+            token_type_tile = psum.tile([P, 1], F32, name=f"token_type{block}")
+            nc.tensor.matmul(token_type_tile[:], type_row[:, channels], one[:], start=True, stop=True)
+            token_type = token_type_tile[:, 0:1]
 
-            group = SEQUENCES if block == 0 else 1
-
-            positional = held.tile([P, group * SEQ_LEN], F32, name=f"positional{block}")
-            for seq in range(group):
+            repeats = max(PIECES[block]) // SEQ_LEN
+            positional = held.tile([P, repeats * SEQ_LEN], F32, name=f"positional{block}")
+            for repeat in range(repeats):
                 nc.vector.tensor_scalar_add(
-                    positional[:, seq * SEQ_LEN : (seq + 1) * SEQ_LEN], position[:], token_type[:, 0:1]
+                    positional[:, repeat * SEQ_LEN : (repeat + 1) * SEQ_LEN], position, token_type
                 )
 
-            for first in range(0, SEQUENCES, group):
-                embedded = results.tile([P, group * SEQ_LEN], F32, name=f"embedded{group}")
+            first = 0
+            for entries in PIECES[block]:
+                start = first % SEQ_LEN
+                embedded = results.tile([P, entries], F32, name=f"embedded{block}_{first}")
                 nc.vector.tensor_tensor(
                     embedded[:],
-                    table[:].indirect(offsets[:, first * SEQ_COLS : (first + group) * SEQ_COLS]),
-                    positional[:],
+                    table[:].indirect(offsets[:, first // OFFS_PER_COL : (first + entries) // OFFS_PER_COL]),
+                    positional[:, start : start + entries],
                     ADD,
                 )
-                nc.scalar.dma_start(out[channels, first * SEQ_LEN : (first + group) * SEQ_LEN], embedded[:])
+                nc.scalar.dma_start(out[channels, first : first + entries], embedded[:])
+                first += entries

@@ -17,7 +17,6 @@ SEQ_COLS = SEQ_LEN // OFFS_PER_COL
 FLOPS = 2 * CHANNELS * TOKENS
 
 PIECES = [[TOKENS], [TOKENS // 2, TOKENS // 4, TOKENS // 8, TOKENS // 16, TOKENS // 16]]
-TABLE_LOADS = [4, 1]
 
 
 def tile_enhancedtransformertextclassifier_kernel(tc, tok, pos, typ, offs, out):
@@ -27,35 +26,35 @@ def tile_enhancedtransformertextclassifier_kernel(tc, tok, pos, typ, offs, out):
         tc.tile_pool(name="results", bufs=1) as results,
         tc.psum_pool(name="psum", bufs=1) as psum,
     ):
+        tables = [held.tile([P, VOCAB], F32, name=f"table{block}") for block in range(BLOCKS)]
         offsets = held.tile([P, TOKENS // OFFS_PER_COL], U16, name="offsets")
-        nc.sync.dma_start(offsets[:], offs)
-
         type_row = held.tile([1, CHANNELS], F32, name="type_row")
-        nc.scalar.dma_start(type_row[:], typ.rearrange("c o -> o c"))
+        positions = held.tile([P, BLOCKS, SEQ_LEN], F32, name="positions")
+
+        first_half, second_half = slice(0, VOCAB // 2), slice(VOCAB // 2, VOCAB)
+        nc.sync.dma_start(tables[0][:, first_half], tok[0:P, first_half])
+        nc.sync.dma_start(offsets[:], offs)
+        nc.sync.dma_start(type_row[:], typ.rearrange("c o -> o c"))
+        nc.sync.dma_start(positions[:], pos.rearrange("(b p) t -> p b t", p=P))
+        nc.sync.dma_start(tables[0][:, second_half], tok[0:P, second_half])
+        nc.sync.dma_start(tables[1][:], tok[P:CHANNELS, :])
+
         one = held.tile([1, 1], F32, name="one")
         nc.vector.memset(one[:], 1.0)
 
         for block in range(BLOCKS):
             channels = slice(block * P, (block + 1) * P)
 
-            table = held.tile([P, VOCAB], F32, name=f"table{block}")
-            width = VOCAB // TABLE_LOADS[block]
-            for load in range(TABLE_LOADS[block]):
-                words = slice(load * width, (load + 1) * width)
-                nc.sync.dma_start(table[:, words], tok[channels, words])
-
-            position_tile = held.tile([P, SEQ_LEN], F32, name=f"position{block}")
-            nc.scalar.dma_start(position_tile[:], pos[channels, :])
-            position = position_tile[:]
-            token_type_tile = psum.tile([P, 1], F32, name=f"token_type{block}")
-            nc.tensor.matmul(token_type_tile[:], type_row[:, channels], one[:], start=True, stop=True)
-            token_type = token_type_tile[:, 0:1]
+            token_type = psum.tile([P, 1], F32, name=f"token_type{block}")
+            nc.tensor.matmul(token_type[:], type_row[:, channels], one[:], start=True, stop=True)
 
             repeats = max(PIECES[block]) // SEQ_LEN
             positional = held.tile([P, repeats * SEQ_LEN], F32, name=f"positional{block}")
             for repeat in range(repeats):
                 nc.vector.tensor_scalar_add(
-                    positional[:, repeat * SEQ_LEN : (repeat + 1) * SEQ_LEN], position, token_type
+                    positional[:, repeat * SEQ_LEN : (repeat + 1) * SEQ_LEN],
+                    positions[:, block, :],
+                    token_type[:, 0:1],
                 )
 
             first = 0
@@ -64,7 +63,7 @@ def tile_enhancedtransformertextclassifier_kernel(tc, tok, pos, typ, offs, out):
                 embedded = results.tile([P, entries], F32, name=f"embedded{block}_{first}")
                 nc.vector.tensor_tensor(
                     embedded[:],
-                    table[:].indirect(offsets[:, first // OFFS_PER_COL : (first + entries) // OFFS_PER_COL]),
+                    tables[block][:].indirect(offsets[:, first // OFFS_PER_COL : (first + entries) // OFFS_PER_COL]),
                     positional[:, start : start + entries],
                     ADD,
                 )

@@ -26,27 +26,28 @@ def tile_enhancedtransformertextclassifier_kernel(tc, tok, pos, typ, offs, out):
         tc.tile_pool(name="results", bufs=1) as results,
         tc.psum_pool(name="psum", bufs=1) as psum,
     ):
+        tok_blocks = tok.rearrange("(p b) v -> p b v", b=BLOCKS)
+        out_blocks = out.rearrange("(p b) j -> p b j", b=BLOCKS)
+
         tables = [held.tile([P, VOCAB], F32, name=f"table{block}") for block in range(BLOCKS)]
         offsets = held.tile([P, TOKENS // OFFS_PER_COL], U16, name="offsets")
         type_row = held.tile([1, CHANNELS], F32, name="type_row")
         positions = held.tile([P, BLOCKS, SEQ_LEN], F32, name="positions")
 
         first_half, second_half = slice(0, VOCAB // 2), slice(VOCAB // 2, VOCAB)
-        nc.sync.dma_start(tables[0][:, first_half], tok[0:P, first_half])
+        nc.sync.dma_start(tables[0][:, first_half], tok_blocks[:, 0, first_half])
         nc.sync.dma_start(offsets[:], offs)
         nc.sync.dma_start(type_row[:], typ.rearrange("c o -> o c"))
-        nc.sync.dma_start(positions[:], pos.rearrange("(b p) t -> p b t", p=P))
-        nc.sync.dma_start(tables[0][:, second_half], tok[0:P, second_half])
-        nc.sync.dma_start(tables[1][:], tok[P:CHANNELS, :])
+        nc.sync.dma_start(positions[:], pos.rearrange("(p b) t -> p b t", b=BLOCKS))
+        nc.sync.dma_start(tables[0][:, second_half], tok_blocks[:, 0, second_half])
+        nc.sync.dma_start(tables[1][:], tok_blocks[:, 1, :])
 
         one = held.tile([1, 1], F32, name="one")
         nc.vector.memset(one[:], 1.0)
 
         for block in range(BLOCKS):
-            channels = slice(block * P, (block + 1) * P)
-
             token_type = psum.tile([P, 1], F32, name=f"token_type{block}")
-            nc.tensor.matmul(token_type[:], type_row[:, channels], one[:], start=True, stop=True)
+            nc.tensor.matmul(token_type[:], type_row[:, block::BLOCKS], one[:], start=True, stop=True)
 
             repeats = max(PIECES[block]) // SEQ_LEN
             positional = held.tile([P, repeats * SEQ_LEN], F32, name=f"positional{block}")
@@ -67,5 +68,5 @@ def tile_enhancedtransformertextclassifier_kernel(tc, tok, pos, typ, offs, out):
                     positional[:, start : start + entries],
                     ADD,
                 )
-                nc.scalar.dma_start(out[channels, first : first + entries], embedded[:])
+                nc.scalar.dma_start(out_blocks[:, block, first : first + entries], embedded[:])
                 first += entries

@@ -34,13 +34,11 @@ def tile_enhancedtransformertextclassifier_kernel(tc, tok, pos, typ, offs, out):
         type_row = held.tile([1, CHANNELS], F32, name="type_row")
         positions = held.tile([P, BLOCKS, SEQ_LEN], F32, name="positions")
 
-        first_half, second_half = slice(0, VOCAB // 2), slice(VOCAB // 2, VOCAB)
-        nc.sync.dma_start(tables[0][:, first_half], tok_blocks[:, 0, first_half])
+        nc.sync.dma_start(positions[:], pos.rearrange("(p b) t -> p b t", b=BLOCKS))
         nc.sync.dma_start(offsets[:], offs)
         nc.sync.dma_start(type_row[:], typ.rearrange("c o -> o c"))
-        nc.sync.dma_start(positions[:], pos.rearrange("(p b) t -> p b t", b=BLOCKS))
-        nc.sync.dma_start(tables[0][:, second_half], tok_blocks[:, 0, second_half])
-        nc.sync.dma_start(tables[1][:], tok_blocks[:, 1, :])
+        for block in range(BLOCKS):
+            nc.sync.dma_start(tables[block][:], tok_blocks[:, block, :])
 
         one = held.tile([1, 1], F32, name="one")
         nc.vector.memset(one[:], 1.0)

@@ -3,6 +3,7 @@ import concourse.mybir as mybir
 F32 = mybir.dt.float32
 U16 = mybir.dt.uint16
 ADD = mybir.AluOpType.add
+IDENTITY = mybir.ActivationFunctionType.Identity
 
 P = 128
 CHANNELS = 256
@@ -32,13 +33,15 @@ def tile_enhancedtransformertextclassifier_kernel(tc, tok, pos, typ, offs, out):
         tables = [held.tile([P, VOCAB], F32, name=f"table{block}") for block in range(BLOCKS)]
         offsets = held.tile([P, TOKENS // OFFS_PER_COL], U16, name="offsets")
         type_row = held.tile([1, CHANNELS], F32, name="type_row")
-        positions = held.tile([P, BLOCKS, SEQ_LEN], F32, name="positions")
+        positions = [held.tile([P, SEQ_LEN], F32, name=f"position{block}") for block in range(BLOCKS)]
 
-        nc.sync.dma_start(positions[:], pos.rearrange("(p b) t -> p b t", b=BLOCKS))
+        pos_blocks = pos.rearrange("(p b) t -> p b t", b=BLOCKS)
+        nc.sync.dma_start(positions[0][:], pos_blocks[:, 0, :])
         nc.sync.dma_start(offsets[:], offs)
         nc.sync.dma_start(type_row[:], typ.rearrange("c o -> o c"))
-        for block in range(BLOCKS):
-            nc.sync.dma_start(tables[block][:], tok_blocks[:, block, :])
+        nc.sync.dma_start(tables[0][:], tok_blocks[:, 0, :])
+        nc.sync.dma_start(positions[1][:], pos_blocks[:, 1, :])
+        nc.sync.dma_start(tables[1][:], tok_blocks[:, 1, :])
 
         one = held.tile([1, 1], F32, name="one")
         nc.vector.memset(one[:], 1.0)
@@ -49,12 +52,15 @@ def tile_enhancedtransformertextclassifier_kernel(tc, tok, pos, typ, offs, out):
 
             repeats = max(PIECES[block]) // SEQ_LEN
             positional = held.tile([P, repeats * SEQ_LEN], F32, name=f"positional{block}")
+            if block == 1:
+                bias = held.tile([P, 1], F32, name="bias")
+                nc.scalar.copy(bias[:], token_type[:])
             for repeat in range(repeats):
-                nc.vector.tensor_scalar_add(
-                    positional[:, repeat * SEQ_LEN : (repeat + 1) * SEQ_LEN],
-                    positions[:, block, :],
-                    token_type[:, 0:1],
-                )
+                repeated = positional[:, repeat * SEQ_LEN : (repeat + 1) * SEQ_LEN]
+                if block == 0:
+                    nc.vector.tensor_scalar_add(repeated, positions[block][:], token_type[:, 0:1])
+                else:
+                    nc.scalar.activation(repeated, positions[block][:], IDENTITY, bias=bias[:])
 
             first = 0
             for entries in PIECES[block]:

import concourse.mybir as mybir

F32 = mybir.dt.float32
U16 = mybir.dt.uint16
ADD = mybir.AluOpType.add
IDENTITY = mybir.ActivationFunctionType.Identity

P = 128
CHANNELS = 256
BLOCKS = CHANNELS // P
VOCAB = 2048
SEQ_LEN = 256
SEQUENCES = 4
TOKENS = SEQUENCES * SEQ_LEN
OFFS_PER_COL = 16
SEQ_COLS = SEQ_LEN // OFFS_PER_COL

FLOPS = 2 * CHANNELS * TOKENS

PIECES = [[TOKENS], [TOKENS // 2, TOKENS // 4, TOKENS // 8, TOKENS // 16, TOKENS // 16]]


def tile_enhancedtransformertextclassifier_kernel(tc, tok, pos, typ, offs, out):
    nc = tc.nc
    with (
        tc.tile_pool(name="held", bufs=1) as held,
        tc.tile_pool(name="results", bufs=1) as results,
        tc.psum_pool(name="psum", bufs=1) as psum,
    ):
        tok_blocks = tok.rearrange("(p b) v -> p b v", b=BLOCKS)
        out_blocks = out.rearrange("(p b) j -> p b j", b=BLOCKS)

        tables = [held.tile([P, VOCAB], F32, name=f"table{block}") for block in range(BLOCKS)]
        offsets = held.tile([P, TOKENS // OFFS_PER_COL], U16, name="offsets")
        type_row = held.tile([1, CHANNELS], F32, name="type_row")
        positions = [held.tile([P, SEQ_LEN], F32, name=f"position{block}") for block in range(BLOCKS)]

        pos_blocks = pos.rearrange("(p b) t -> p b t", b=BLOCKS)
        nc.sync.dma_start(positions[0][:], pos_blocks[:, 0, :])
        nc.sync.dma_start(offsets[:], offs)
        nc.sync.dma_start(type_row[:], typ.rearrange("c o -> o c"))
        nc.sync.dma_start(tables[0][:], tok_blocks[:, 0, :])
        nc.sync.dma_start(positions[1][:], pos_blocks[:, 1, :])
        nc.sync.dma_start(tables[1][:], tok_blocks[:, 1, :])

        one = held.tile([1, 1], F32, name="one")
        nc.vector.memset(one[:], 1.0)

        for block in range(BLOCKS):
            token_type = psum.tile([P, 1], F32, name=f"token_type{block}")
            nc.tensor.matmul(token_type[:], type_row[:, block::BLOCKS], one[:], start=True, stop=True)

            repeats = max(PIECES[block]) // SEQ_LEN
            positional = held.tile([P, repeats * SEQ_LEN], F32, name=f"positional{block}")
            if block == 1:
                bias = held.tile([P, 1], F32, name="bias")
                nc.scalar.copy(bias[:], token_type[:])
            for repeat in range(repeats):
                repeated = positional[:, repeat * SEQ_LEN : (repeat + 1) * SEQ_LEN]
                if block == 0:
                    nc.vector.tensor_scalar_add(repeated, positions[block][:], token_type[:, 0:1])
                else:
                    nc.scalar.activation(repeated, positions[block][:], IDENTITY, bias=bias[:])

            first = 0
            for entries in PIECES[block]:
                start = first % SEQ_LEN
                embedded = results.tile([P, entries], F32, name=f"embedded{block}_{first}")
                nc.vector.tensor_tensor(
                    embedded[:],
                    tables[block][:].indirect(offsets[:, first // OFFS_PER_COL : (first + entries) // OFFS_PER_COL]),
                    positional[:, start : start + entries],
                    ADD,
                )
                nc.scalar.dma_start(out_blocks[:, block, first : first + entries], embedded[:])
                first += entries
